import numpy as np
import ml_dtypes


def mxq(x, axis, fmt="e4m3"):
    dtype, down = {"e4m3": (ml_dtypes.float8_e4m3fn, 7), "e5m2": (ml_dtypes.float8_e5m2, 14)}[fmt]
    v = np.moveaxis(np.asarray(x, np.float32).astype(ml_dtypes.bfloat16).astype(np.float64), axis, -1)
    blocks = v.reshape(v.shape[:-1] + (-1, 32))
    amax = np.abs(blocks).max(-1, keepdims=True)
    byte = np.maximum(np.where(amax > 0, np.frexp(amax)[1] - 1 + 127, 0) - down, 1)
    scale = np.exp2(byte - 127.0)
    codes = (blocks / scale).astype(np.float32).astype(dtype).astype(np.float64)
    return np.moveaxis((codes * scale).reshape(v.shape), -1, axis)


BF16 = ml_dtypes.bfloat16


def bf(x):
    return np.asarray(x, np.float32).astype(BF16)


def f64(x):
    return np.asarray(x).astype(np.float64)


B, IN, OUT, ND, R = 8192, 512, 64, 8, 4


def setup_inputs():
    p = np.random.standard_normal((R, IN)) / np.sqrt(IN)
    a = np.sqrt(2.0 / R)
    x = np.random.standard_normal((B, R)) @ p * a
    centers = (np.random.standard_normal((OUT * ND, R)) @ p * a).reshape(OUT, ND, IN)
    return {"x": bf(x), "centers": bf(centers)}


def reference(x, centers):
    x = f64(x)
    centers = f64(centers)
    O, D, F = centers.shape
    c = centers.reshape(O * D, F)
    x2 = np.sum(x * x, axis=-1, keepdims=True)
    c2 = np.sum(c * c, axis=-1)[None, :]
    d2 = x2 - 2.0 * (mxq(x, 1, "e4m3") @ mxq(c, 1, "e4m3").T) + c2
    sigma = 1.0
    probs = np.exp(-d2 / (2.0 * sigma * sigma)).reshape(-1, O, D)
    out = (np.max(probs, axis=-1) * (D + 1) - np.sum(probs, axis=-1)) / D
    return out

@@ -1,0 +1,144 @@
+import math
+from contextlib import ExitStack
+
+import concourse.mybir as mybir
+from concourse.masks import make_identity
+
+F32 = mybir.dt.float32
+BF16 = mybir.dt.bfloat16
+U32 = mybir.dt.uint32
+U8 = mybir.dt.uint8
+FP8X4 = mybir.dt.float8_e4m3fn_x4
+ALU = mybir.AluOpType
+ACT = mybir.ActivationFunctionType
+AX = mybir.AxisListType
+
+P = 128
+B, K, J, O, D = 8192, 512, 512, 64, 8
+NT = B // P
+QUAD = 4
+NQ = NT // QUAD
+FLOPS = 2 * B * K * J
+LN8 = math.log(8.0)
+RH = math.sqrt(0.5)
+CHUNKS = [4, 4, 8, 8, 8, 8, 8, 8, 8]
+VCOPY_EVERY = 4
+
+
+def tile_pnn_t_kernel(tc, x, centers, out):
+    nc = tc.nc
+    xv = x.rearrange("(p t) k -> p (t k)", t=NT)
+    cv = centers.rearrange("o d k -> (o d) k").rearrange("(i r) k -> r i k", r=P)
+    ov = out.rearrange("(p t) o -> p (t o)", t=NT)
+
+    with ExitStack() as ctx:
+        const = ctx.enter_context(tc.tile_pool(name="const", bufs=1))
+        xpool = ctx.enter_context(tc.tile_pool(name="xpool", bufs=1))
+        gpool = ctx.enter_context(tc.tile_pool(name="gpool", bufs=3))
+        wpool = ctx.enter_context(tc.tile_pool(name="wpool", bufs=3))
+        spool = ctx.enter_context(tc.tile_pool(name="spool", bufs=2))
+        ps_t = ctx.enter_context(tc.psum_pool(name="ps_t", bufs=3))
+        ps_m = ctx.enter_context(tc.psum_pool(name="ps_m", bufs=5))
+
+        c_sb = const.tile([P, 4 * K], BF16, name="c_sb")
+        nc.sync.dma_start(out=c_sb[:].rearrange("r (i k) -> r i k", i=4), in_=cv)
+        quad_src = []
+        t0 = 0
+        for ci, n in enumerate(CHUNKS):
+            xc = xpool.tile([P, n * K], BF16, name="x%d" % ci)
+            nc.sync.dma_start(out=xc[:], in_=xv[:, t0 * K:(t0 + n) * K])
+            for h in range(n // QUAD):
+                quad_src.append(xc[:, h * QUAD * K:(h + 1) * QUAD * K])
+            t0 += n
+
+        ident = const.tile([P, P], F32, name="ident")
+        make_identity(nc, ident[:])
+        ones = const.tile([P, P], F32, name="ones")
+        nc.vector.memset(ones[:], 1.0)
+
+        counter = [0]
+
+        def pack_quad(src):
+            src32 = src.bitcast(F32)
+            g = gpool.tile([P, QUAD * K], BF16, align_bytes=64, tag="g", name="g")
+            g32 = g[:].bitcast(F32)
+            for h in range(2):
+                xt = ps_t.tile([P, 512], F32, tag="xt", name="xt")
+                for c in range(2):
+                    for u in range(2):
+                        col = (2 * h + c) * 256 + u * P
+                        nc.tensor.transpose(xt[:, (2 * c + u) * P:(2 * c + u + 1) * P], src32[:, col:col + P], ident[:])
+                dst = g32[:, h * 512:(h + 1) * 512].rearrange("p (c b u) -> p c b u", c=2, u=2)
+                srcv = xt[:].rearrange("p (c u b) -> p c b u", c=2, u=2)
+                if counter[0] % VCOPY_EVERY == VCOPY_EVERY - 1:
+                    nc.vector.tensor_copy(out=dst, in_=srcv)
+                else:
+                    nc.scalar.copy(out=dst, in_=srcv)
+                counter[0] += 1
+            return g
+
+        def half_norms(src, dest, n):
+            for i in range(n):
+                junk = spool.tile([P, K], BF16, tag="junk", name="junk")
+                nc.scalar.activation(out=junk[:], in_=src[:, i * K:(i + 1) * K], func=ACT.Square, scale=RH,
+                                     accum_out=dest[:, i:i + 1])
+
+        c_codes = const.tile([P, J], U32, align_bytes=64, name="c_codes")
+        c_scales = const.tile([P, J], U8, align_bytes=64, name="c_scales")
+        cg = pack_quad(c_sb[:])
+        nc.vector.quantize_mx(out=c_codes[:].bitcast(FP8X4), scales=c_scales[:], in_=cg[:])
+        c2h = const.tile([P, 4], F32, name="c2h")
+        half_norms(c_sb[:], c2h, 4)
+        c_rep = const.tile([P, 4 * P], F32, name="c_rep")
+        cb_ps = ps_m.tile([P, J], F32, tag="mm", name="cb_ps")
+        for i in range(4):
+            nc.vector.tensor_scalar_mul(out=c_rep[:, i * P:(i + 1) * P], in0=ones[:], scalar1=c2h[:, i:i + 1])
+            nc.tensor.transpose(cb_ps[:, i * P:(i + 1) * P], c_rep[:, i * P:(i + 1) * P], ident[:])
+        c2b = const.tile([P, J], F32, name="c2b")
+        nc.vector.tensor_scalar(out=c2b[:], in0=cb_ps[:], scalar1=-1.0, scalar2=-LN8, op0=ALU.mult, op1=ALU.add)
+
+        x2h = const.tile([P, NT], F32, name="x2h")
+
+        def prep(q):
+            half_norms(quad_src[q], x2h[:, q * QUAD:(q + 1) * QUAD], QUAD)
+            return pack_quad(quad_src[q])
+
+        g_next = prep(0)
+        o_sb = None
+        for q in range(NQ):
+            g = g_next
+            codes = wpool.tile([P, QUAD * P], U32, align_bytes=64, tag="codes", name="codes")
+            scales = wpool.tile([P, QUAD * P], U8, align_bytes=64, tag="scales", name="scales")
+            nc.vector.quantize_mx(out=codes[:].bitcast(FP8X4), scales=scales[:], in_=g[:])
+            if q + 1 < NQ:
+                g_next = prep(q + 1)
+            t_sb = wpool.tile([P, QUAD * J], F32, tag="t", name="t_sb")
+            for i in range(QUAD):
+                mm = ps_m.tile([P, J], F32, tag="mm", name="mm")
+                nc.tensor.matmul_mx(out=mm[:], lhsT=codes[:, i * P:(i + 1) * P].bitcast(FP8X4),
+                                    lhsT_scale=scales[:, i * P:(i + 1) * P],
+                                    rhs=c_codes[:].bitcast(FP8X4), rhs_scale=c_scales[:], start=True, stop=True)
+                t = q * QUAD + i
+                nc.vector.scalar_tensor_tensor(out=t_sb[:, i * J:(i + 1) * J], in0=mm[:], scalar=x2h[:, t:t + 1],
+                                               in1=c2b[:], op0=ALU.subtract, op1=ALU.add)
+            p_sb = wpool.tile([P, QUAD * J], F32, tag="p", name="p_sb")
+            nc.scalar.activation(out=p_sb[:], in_=t_sb[:], func=ACT.Exp)
+            p3 = p_sb[:].rearrange("p (g d) -> p g d", d=8)
+            mx = spool.tile([P, QUAD * O], F32, tag="mx", name="mx")
+            nc.vector.tensor_reduce(out=mx[:], in_=p3, axis=AX.X, op=ALU.max)
+            l1 = spool.tile([P, QUAD * O * 4], F32, tag="l1", name="l1")
+            l1v = l1[:].rearrange("p (g d) -> p g d", d=4)
+            nc.gpsimd.tensor_tensor(out=l1v, in0=p3[:, :, 0:4], in1=p3[:, :, 4:8], op=ALU.add)
+            l2 = spool.tile([P, QUAD * O * 2], F32, tag="l2", name="l2")
+            l2v = l2[:].rearrange("p (g d) -> p g d", d=2)
+            nc.gpsimd.tensor_tensor(out=l2v, in0=l1v[:, :, 0:2], in1=l1v[:, :, 2:4], op=ALU.add)
+            l3 = spool.tile([P, QUAD * O], F32, tag="l3", name="l3")
+            l3v = l3[:].rearrange("p (g d) -> p g d", d=1)
+            nc.gpsimd.tensor_tensor(out=l3v, in0=l2v[:, :, 0:1], in1=l2v[:, :, 1:2], op=ALU.add)
+            if q % 2 == 0:
+                o_sb = spool.tile([P, 2 * QUAD * O], F32, tag="o", name="o_sb")
+            w = QUAD * O
+            nc.vector.scalar_tensor_tensor(out=o_sb[:, (q % 2) * w:(q % 2 + 1) * w], in0=mx[:], scalar=9.0, in1=l3[:],
+                                           op0=ALU.mult, op1=ALU.subtract)
+            if q % 2 == 1:
+                nc.sync.dma_start(out=ov[:, (q - 1) * w:(q + 1) * w], in_=o_sb[:])

@@ -22,7 +22,11 @@ FLOPS = 2 * B * K * J
 LN8 = math.log(8.0)
 RH = math.sqrt(0.5)
 CHUNKS = [4, 4, 8, 8, 8, 8, 8, 8, 8]
-VCOPY_EVERY = 4
+X2_AHEAD = 3
+
+
+def vector_copies(q, h):
+    return q == 0 and h == 1
 
 
 def tile_pnn_t_kernel(tc, x, centers, out):
@@ -32,11 +36,12 @@ def tile_pnn_t_kernel(tc, x, centers, out):
     ov = out.rearrange("(p t) o -> p (t o)", t=NT)
 
     with ExitStack() as ctx:
+        ctx.enter_context(tc.manual_schedule())
         const = ctx.enter_context(tc.tile_pool(name="const", bufs=1))
         xpool = ctx.enter_context(tc.tile_pool(name="xpool", bufs=1))
         gpool = ctx.enter_context(tc.tile_pool(name="gpool", bufs=3))
         wpool = ctx.enter_context(tc.tile_pool(name="wpool", bufs=3))
-        spool = ctx.enter_context(tc.tile_pool(name="spool", bufs=2))
+        spool = ctx.enter_context(tc.tile_pool(name="spool", bufs=3))
         ps_t = ctx.enter_context(tc.psum_pool(name="ps_t", bufs=3))
         ps_m = ctx.enter_context(tc.psum_pool(name="ps_m", bufs=5))
 
@@ -55,26 +60,31 @@ def tile_pnn_t_kernel(tc, x, centers, out):
         make_identity(nc, ident[:])
         ones = const.tile([P, P], F32, name="ones")
         nc.vector.memset(ones[:], 1.0)
+        x2h = const.tile([P, NT], F32, name="x2h")
+        c2h = const.tile([P, 4], F32, name="c2h")
 
-        counter = [0]
-
-        def pack_quad(src):
+        def transposes(src):
             src32 = src.bitcast(F32)
-            g = gpool.tile([P, QUAD * K], BF16, align_bytes=64, tag="g", name="g")
-            g32 = g[:].bitcast(F32)
+            banks = []
             for h in range(2):
                 xt = ps_t.tile([P, 512], F32, tag="xt", name="xt")
                 for c in range(2):
                     for u in range(2):
                         col = (2 * h + c) * 256 + u * P
                         nc.tensor.transpose(xt[:, (2 * c + u) * P:(2 * c + u + 1) * P], src32[:, col:col + P], ident[:])
+                banks.append(xt)
+            return banks
+
+        def copies(banks, on_vector):
+            g = gpool.tile([P, QUAD * K], BF16, align_bytes=64, tag="g", name="g")
+            g32 = g[:].bitcast(F32)
+            for h in range(2):
                 dst = g32[:, h * 512:(h + 1) * 512].rearrange("p (c b u) -> p c b u", c=2, u=2)
-                srcv = xt[:].rearrange("p (c u b) -> p c b u", c=2, u=2)
-                if counter[0] % VCOPY_EVERY == VCOPY_EVERY - 1:
+                srcv = banks[h][:].rearrange("p (c u b) -> p c b u", c=2, u=2)
+                if on_vector[h]:
                     nc.vector.tensor_copy(out=dst, in_=srcv)
                 else:
                     nc.scalar.copy(out=dst, in_=srcv)
-                counter[0] += 1
             return g
 
         def half_norms(src, dest, n):
@@ -83,62 +93,135 @@ def tile_pnn_t_kernel(tc, x, centers, out):
                 nc.scalar.activation(out=junk[:], in_=src[:, i * K:(i + 1) * K], func=ACT.Square, scale=RH,
                                      accum_out=dest[:, i:i + 1])
 
+        def norms_x(q):
+            if q < NQ:
+                half_norms(quad_src[q], x2h[:, q * QUAD:(q + 1) * QUAD], QUAD)
+
+        half_norms(c_sb[:], c2h, 4)
+        c_banks = transposes(c_sb[:])
+        cg = copies(c_banks, [True, True])
         c_codes = const.tile([P, J], U32, align_bytes=64, name="c_codes")
         c_scales = const.tile([P, J], U8, align_bytes=64, name="c_scales")
-        cg = pack_quad(c_sb[:])
         nc.vector.quantize_mx(out=c_codes[:].bitcast(FP8X4), scales=c_scales[:], in_=cg[:])
-        c2h = const.tile([P, 4], F32, name="c2h")
-        half_norms(c_sb[:], c2h, 4)
+
+        banks = {}
+        grouped = {}
+        packed = {}
+        products = {}
+        logits = {}
+        probs = {}
+        maxes = {}
+        sums = {}
+
+        def do_transposes(q):
+            if q < NQ:
+                banks[q] = transposes(quad_src[q])
+
+        def do_copies(q):
+            if q < NQ:
+                grouped[q] = copies(banks[q], [vector_copies(q, 0), vector_copies(q, 1)])
+
+        def do_quantise(q):
+            if q < NQ:
+                codes = wpool.tile([P, QUAD * P], U32, align_bytes=64, tag="codes", name="codes")
+                scales = wpool.tile([P, QUAD * P], U8, align_bytes=64, tag="scales", name="scales")
+                nc.vector.quantize_mx(out=codes[:].bitcast(FP8X4), scales=scales[:], in_=grouped[q][:])
+                packed[q] = (codes, scales)
+
+        def do_products(q):
+            if q < NQ:
+                codes, scales = packed[q]
+                products[q] = []
+                for i in range(QUAD):
+                    mm = ps_m.tile([P, J], F32, tag="mm", name="mm")
+                    nc.tensor.matmul_mx(out=mm[:], lhsT=codes[:, i * P:(i + 1) * P].bitcast(FP8X4),
+                                        lhsT_scale=scales[:, i * P:(i + 1) * P],
+                                        rhs=c_codes[:].bitcast(FP8X4), rhs_scale=c_scales[:], start=True, stop=True)
+                    products[q].append(mm)
+
+        def units(q):
+            if q == NQ - 1:
+                return [(0, 1), (1, 1), (2, 1), (3, 1)]
+            return [(0, 4)]
+
+        def do_logits_exp(q):
+            logits[q] = []
+            probs[q] = []
+            for (i0, n) in units(q):
+                t_sb = wpool.tile([P, n * J], F32, tag="t%d" % n, name="t_sb", bufs=(3 if n == QUAD else 4))
+                for i in range(n):
+                    t = q * QUAD + i0 + i
+                    nc.vector.scalar_tensor_tensor(out=t_sb[:, i * J:(i + 1) * J], in0=products[q][i0 + i][:],
+                                                   scalar=x2h[:, t:t + 1], in1=c2b[:], op0=ALU.subtract, op1=ALU.add)
+                logits[q].append(t_sb)
+                if n < QUAD:
+                    do_exp(q, len(logits[q]) - 1)
+
+        def do_exp(q, ui):
+            n = units(q)[ui][1]
+            p_sb = wpool.tile([P, n * J], F32, tag="p%d" % n, name="p_sb", bufs=(3 if n == QUAD else 4))
+            nc.scalar.activation(out=p_sb[:], in_=logits[q][ui][:], func=ACT.Exp)
+            probs[q].append(p_sb)
+
+        def do_reduce(q):
+            maxes[q] = []
+            sums[q] = []
+            nu = len(units(q))
+            for ui, (i0, n) in enumerate(units(q)):
+                p3 = probs[q][ui][:].rearrange("p (g d) -> p g d", d=8)
+                mx = spool.tile([P, n * O], F32, tag="mx", name="mx", bufs=6)
+                nc.vector.tensor_reduce(out=mx[:], in_=p3, axis=AX.X, op=ALU.max)
+                l3 = spool.tile([P, n * O], F32, tag="l3", name="l3", bufs=6)
+                if nu > 1 and ui >= 2:
+                    nc.vector.tensor_reduce(out=l3[:], in_=p3, axis=AX.X, op=ALU.add)
+                else:
+                    l1 = spool.tile([P, n * O * 4], F32, tag="l1", name="l1", bufs=2)
+                    l1v = l1[:].rearrange("p (g d) -> p g d", d=4)
+                    nc.gpsimd.tensor_tensor(out=l1v, in0=p3[:, :, 0:4], in1=p3[:, :, 4:8], op=ALU.add)
+                    l2 = spool.tile([P, n * O * 2], F32, tag="l2", name="l2", bufs=2)
+                    l2v = l2[:].rearrange("p (g d) -> p g d", d=2)
+                    nc.gpsimd.tensor_tensor(out=l2v, in0=l1v[:, :, 0:2], in1=l1v[:, :, 2:4], op=ALU.add)
+                    l3v = l3[:].rearrange("p (g d) -> p g d", d=1)
+                    nc.gpsimd.tensor_tensor(out=l3v, in0=l2v[:, :, 0:1], in1=l2v[:, :, 1:2], op=ALU.add)
+                maxes[q].append(mx)
+                sums[q].append(l3)
+
+        def do_final(q):
+            o_sb = spool.tile([P, QUAD * O], F32, tag="o", name="o_sb")
+            for ui, (i0, n) in enumerate(units(q)):
+                nc.vector.scalar_tensor_tensor(out=o_sb[:, i0 * O:(i0 + n) * O], in0=maxes[q][ui][:], scalar=9.0,
+                                               in1=sums[q][ui][:], op0=ALU.mult, op1=ALU.subtract)
+            w = QUAD * O
+            nc.sync.dma_start(out=ov[:, q * w:(q + 1) * w], in_=o_sb[:])
+
+        do_transposes(0)
         c_rep = const.tile([P, 4 * P], F32, name="c_rep")
         cb_ps = ps_m.tile([P, J], F32, tag="mm", name="cb_ps")
         for i in range(4):
             nc.vector.tensor_scalar_mul(out=c_rep[:, i * P:(i + 1) * P], in0=ones[:], scalar1=c2h[:, i:i + 1])
             nc.tensor.transpose(cb_ps[:, i * P:(i + 1) * P], c_rep[:, i * P:(i + 1) * P], ident[:])
+        do_copies(0)
+        norms_x(0)
+        do_quantise(0)
         c2b = const.tile([P, J], F32, name="c2b")
         nc.vector.tensor_scalar(out=c2b[:], in0=cb_ps[:], scalar1=-1.0, scalar2=-LN8, op0=ALU.mult, op1=ALU.add)
+        do_transposes(1)
+        do_products(0)
+        do_copies(1)
+        for q in range(1, X2_AHEAD):
+            norms_x(q)
 
-        x2h = const.tile([P, NT], F32, name="x2h")
-
-        def prep(q):
-            half_norms(quad_src[q], x2h[:, q * QUAD:(q + 1) * QUAD], QUAD)
-            return pack_quad(quad_src[q])
-
-        g_next = prep(0)
-        o_sb = None
-        for q in range(NQ):
-            g = g_next
-            codes = wpool.tile([P, QUAD * P], U32, align_bytes=64, tag="codes", name="codes")
-            scales = wpool.tile([P, QUAD * P], U8, align_bytes=64, tag="scales", name="scales")
-            nc.vector.quantize_mx(out=codes[:].bitcast(FP8X4), scales=scales[:], in_=g[:])
-            if q + 1 < NQ:
-                g_next = prep(q + 1)
-            t_sb = wpool.tile([P, QUAD * J], F32, tag="t", name="t_sb")
-            for i in range(QUAD):
-                mm = ps_m.tile([P, J], F32, tag="mm", name="mm")
-                nc.tensor.matmul_mx(out=mm[:], lhsT=codes[:, i * P:(i + 1) * P].bitcast(FP8X4),
-                                    lhsT_scale=scales[:, i * P:(i + 1) * P],
-                                    rhs=c_codes[:].bitcast(FP8X4), rhs_scale=c_scales[:], start=True, stop=True)
-                t = q * QUAD + i
-                nc.vector.scalar_tensor_tensor(out=t_sb[:, i * J:(i + 1) * J], in0=mm[:], scalar=x2h[:, t:t + 1],
-                                               in1=c2b[:], op0=ALU.subtract, op1=ALU.add)
-            p_sb = wpool.tile([P, QUAD * J], F32, tag="p", name="p_sb")
-            nc.scalar.activation(out=p_sb[:], in_=t_sb[:], func=ACT.Exp)
-            p3 = p_sb[:].rearrange("p (g d) -> p g d", d=8)
-            mx = spool.tile([P, QUAD * O], F32, tag="mx", name="mx")
-            nc.vector.tensor_reduce(out=mx[:], in_=p3, axis=AX.X, op=ALU.max)
-            l1 = spool.tile([P, QUAD * O * 4], F32, tag="l1", name="l1")
-            l1v = l1[:].rearrange("p (g d) -> p g d", d=4)
-            nc.gpsimd.tensor_tensor(out=l1v, in0=p3[:, :, 0:4], in1=p3[:, :, 4:8], op=ALU.add)
-            l2 = spool.tile([P, QUAD * O * 2], F32, tag="l2", name="l2")
-            l2v = l2[:].rearrange("p (g d) -> p g d", d=2)
-            nc.gpsimd.tensor_tensor(out=l2v, in0=l1v[:, :, 0:2], in1=l1v[:, :, 2:4], op=ALU.add)
-            l3 = spool.tile([P, QUAD * O], F32, tag="l3", name="l3")
-            l3v = l3[:].rearrange("p (g d) -> p g d", d=1)
-            nc.gpsimd.tensor_tensor(out=l3v, in0=l2v[:, :, 0:1], in1=l2v[:, :, 1:2], op=ALU.add)
-            if q % 2 == 0:
-                o_sb = spool.tile([P, 2 * QUAD * O], F32, tag="o", name="o_sb")
-            w = QUAD * O
-            nc.vector.scalar_tensor_tensor(out=o_sb[:, (q % 2) * w:(q % 2 + 1) * w], in0=mx[:], scalar=9.0, in1=l3[:],
-                                           op0=ALU.mult, op1=ALU.subtract)
-            if q % 2 == 1:
-                nc.sync.dma_start(out=ov[:, (q - 1) * w:(q + 1) * w], in_=o_sb[:])
+        for i in range(NQ + 2):
+            if i < NQ:
+                do_logits_exp(i)
+                do_quantise(i + 1)
+                do_transposes(i + 2)
+                do_products(i + 1)
+                if len(units(i)) == 1:
+                    do_exp(i, 0)
+                do_copies(i + 2)
+                norms_x(i + X2_AHEAD)
+            if 0 <= i - 1 < NQ:
+                do_reduce(i - 1)
+            if 0 <= i - 2 < NQ:
+                do_final(i - 2)

@@ -22,11 +22,16 @@ FLOPS = 2 * B * K * J
 LN8 = math.log(8.0)
 RH = math.sqrt(0.5)
 CHUNKS = [4, 4, 8, 8, 8, 8, 8, 8, 8]
-X2_AHEAD = 3
+CP_AHEAD = 3
+X2_AHEAD = 2
 
 
 def vector_copies(q, h):
-    return q == 0 and h == 1
+    if q == 0:
+        return h == 1
+    if q == 1:
+        return True
+    return h == 1 and q <= 12 and q % 3 == 0
 
 
 def tile_pnn_t_kernel(tc, x, centers, out):
@@ -144,7 +149,9 @@ def tile_pnn_t_kernel(tc, x, centers, out):
                 return [(0, 1), (1, 1), (2, 1), (3, 1)]
             return [(0, 4)]
 
-        def do_logits_exp(q):
+        def do_logits(q):
+            if q >= NQ:
+                return
             logits[q] = []
             probs[q] = []
             for (i0, n) in units(q):
@@ -154,14 +161,14 @@ def tile_pnn_t_kernel(tc, x, centers, out):
                     nc.vector.scalar_tensor_tensor(out=t_sb[:, i * J:(i + 1) * J], in0=products[q][i0 + i][:],
                                                    scalar=x2h[:, t:t + 1], in1=c2b[:], op0=ALU.subtract, op1=ALU.add)
                 logits[q].append(t_sb)
-                if n < QUAD:
-                    do_exp(q, len(logits[q]) - 1)
 
-        def do_exp(q, ui):
-            n = units(q)[ui][1]
-            p_sb = wpool.tile([P, n * J], F32, tag="p%d" % n, name="p_sb", bufs=(3 if n == QUAD else 4))
-            nc.scalar.activation(out=p_sb[:], in_=logits[q][ui][:], func=ACT.Exp)
-            probs[q].append(p_sb)
+        def do_exp(q):
+            if q >= NQ:
+                return
+            for ui, (i0, n) in enumerate(units(q)):
+                p_sb = wpool.tile([P, n * J], F32, tag="p%d" % n, name="p_sb", bufs=(3 if n == QUAD else 4))
+                nc.scalar.activation(out=p_sb[:], in_=logits[q][ui][:], func=ACT.Exp)
+                probs[q].append(p_sb)
 
         def do_reduce(q):
             maxes[q] = []
@@ -208,20 +215,22 @@ def tile_pnn_t_kernel(tc, x, centers, out):
         do_transposes(1)
         do_products(0)
         do_copies(1)
-        for q in range(1, X2_AHEAD):
-            norms_x(q)
+        norms_x(1)
+        do_logits(0)
+        do_quantise(1)
+        do_transposes(2)
+        do_products(1)
+        do_copies(2)
 
-        for i in range(NQ + 2):
-            if i < NQ:
-                do_logits_exp(i)
-                do_quantise(i + 1)
-                do_transposes(i + 2)
-                do_products(i + 1)
-                if len(units(i)) == 1:
-                    do_exp(i, 0)
-                do_copies(i + 2)
-                norms_x(i + X2_AHEAD)
+        for i in range(NQ + 3):
+            do_exp(i)
             if 0 <= i - 1 < NQ:
                 do_reduce(i - 1)
             if 0 <= i - 2 < NQ:
                 do_final(i - 2)
+            do_quantise(i + 2)
+            do_logits(i + 1)
+            do_transposes(i + CP_AHEAD)
+            do_products(i + 2)
+            do_copies(i + CP_AHEAD)
+            norms_x(i + X2_AHEAD)

@@ -27,11 +27,11 @@ X2_AHEAD = 2
 
 
 def vector_copies(q, h):
-    if q == 0:
-        return h == 1
-    if q == 1:
+    if q in (2, 3):
         return True
-    return h == 1 and q <= 12 and q % 3 == 0
+    if q == 0:
+        return h == 0
+    return h == 1 and q in (1, 9, 12)
 
 
 def tile_pnn_t_kernel(tc, x, centers, out):
@@ -51,7 +51,9 @@ def tile_pnn_t_kernel(tc, x, centers, out):
         ps_m = ctx.enter_context(tc.psum_pool(name="ps_m", bufs=5))
 
         c_sb = const.tile([P, 4 * K], BF16, name="c_sb")
-        nc.sync.dma_start(out=c_sb[:].rearrange("r (i k) -> r i k", i=4), in_=cv)
+        for h in range(2):
+            nc.sync.dma_start(out=c_sb[:, h * 2 * K:(h + 1) * 2 * K].rearrange("r (i k) -> r i k", i=2),
+                              in_=cv[:, 2 * h:2 * h + 2, :])
         quad_src = []
         t0 = 0
         for ci, n in enumerate(CHUNKS):
@@ -146,7 +148,7 @@ def tile_pnn_t_kernel(tc, x, centers, out):
 
         def units(q):
             if q == NQ - 1:
-                return [(0, 1), (1, 1), (2, 1), (3, 1)]
+                return [(0, 2), (2, 2)]
             return [(0, 4)]
 
         def do_logits(q):
@@ -179,7 +181,7 @@ def tile_pnn_t_kernel(tc, x, centers, out):
                 mx = spool.tile([P, n * O], F32, tag="mx", name="mx", bufs=6)
                 nc.vector.tensor_reduce(out=mx[:], in_=p3, axis=AX.X, op=ALU.max)
                 l3 = spool.tile([P, n * O], F32, tag="l3", name="l3", bufs=6)
-                if nu > 1 and ui >= 2:
+                if nu > 1 and ui == nu - 1:
                     nc.vector.tensor_reduce(out=l3[:], in_=p3, axis=AX.X, op=ALU.add)
                 else:
                     l1 = spool.tile([P, n * O * 4], F32, tag="l1", name="l1", bufs=2)

@@ -11,27 +11,31 @@ U8 = mybir.dt.uint8
 FP8X4 = mybir.dt.float8_e4m3fn_x4
 ALU = mybir.AluOpType
 ACT = mybir.ActivationFunctionType
-AX = mybir.AxisListType
 
 P = 128
 B, K, J, O, D = 8192, 512, 512, 64, 8
 NT = B // P
 QUAD = 4
 NQ = NT // QUAD
+W = QUAD * O
 FLOPS = 2 * B * K * J
 LN8 = math.log(8.0)
 RH = math.sqrt(0.5)
 CHUNKS = [4, 4, 8, 8, 8, 8, 8, 8, 8]
 CP_AHEAD = 3
 X2_AHEAD = 2
+GRAM_EVEN = [3]
+GRAM_ODD = [3]
+VC = (0, 1)
+VC2 = ()
+
+
+def gram_tiles(q):
+    return GRAM_EVEN if q % 2 == 0 else GRAM_ODD
 
 
 def vector_copies(q, h):
-    if q in (2, 3):
-        return True
-    if q == 0:
-        return h == 0
-    return h == 1 and q in (1, 9, 12)
+    return (h == 0 and q in VC) or (h == 1 and q in VC2)
 
 
 def tile_pnn_t_kernel(tc, x, centers, out):
@@ -48,7 +52,8 @@ def tile_pnn_t_kernel(tc, x, centers, out):
         wpool = ctx.enter_context(tc.tile_pool(name="wpool", bufs=3))
         spool = ctx.enter_context(tc.tile_pool(name="spool", bufs=3))
         ps_t = ctx.enter_context(tc.psum_pool(name="ps_t", bufs=3))
-        ps_m = ctx.enter_context(tc.psum_pool(name="ps_m", bufs=5))
+        ps_m = ctx.enter_context(tc.psum_pool(name="ps_m", bufs=4))
+        ps_s = ctx.enter_context(tc.psum_pool(name="ps_s", bufs=1))
 
         c_sb = const.tile([P, 4 * K], BF16, name="c_sb")
         for h in range(2):
@@ -94,31 +99,37 @@ def tile_pnn_t_kernel(tc, x, centers, out):
                     nc.scalar.copy(out=dst, in_=srcv)
             return g
 
-        def half_norms(src, dest, n):
-            for i in range(n):
+        def half_norms(src, dest, tiles):
+            for i in tiles:
                 junk = spool.tile([P, K], BF16, tag="junk", name="junk")
                 nc.scalar.activation(out=junk[:], in_=src[:, i * K:(i + 1) * K], func=ACT.Square, scale=RH,
                                      accum_out=dest[:, i:i + 1])
 
         def norms_x(q):
             if q < NQ:
-                half_norms(quad_src[q], x2h[:, q * QUAD:(q + 1) * QUAD], QUAD)
-
-        half_norms(c_sb[:], c2h, 4)
-        c_banks = transposes(c_sb[:])
-        cg = copies(c_banks, [True, True])
-        c_codes = const.tile([P, J], U32, align_bytes=64, name="c_codes")
-        c_scales = const.tile([P, J], U8, align_bytes=64, name="c_scales")
-        nc.vector.quantize_mx(out=c_codes[:].bitcast(FP8X4), scales=c_scales[:], in_=cg[:])
+                half_norms(quad_src[q], x2h[:, q * QUAD:(q + 1) * QUAD], [i for i in range(QUAD) if i not in gram_tiles(q)])
 
         banks = {}
         grouped = {}
         packed = {}
         products = {}
+        grams = {}
         logits = {}
         probs = {}
-        maxes = {}
+        tops = {}
         sums = {}
+
+        half_norms(c_sb[:], c2h, range(4))
+        c_banks = transposes(c_sb[:])
+        cg = gpool.tile([P, QUAD * K], BF16, align_bytes=64, tag="g", name="cg")
+        cg_v = cg[:].bitcast(F32).rearrange("p (d c a u) -> p c d a u", d=D, c=4, u=2)
+        for c in range(4):
+            nc.vector.tensor_copy(
+                out=cg_v[:, c],
+                in_=c_banks[c // 2][:, (c % 2) * 256:(c % 2 + 1) * 256].rearrange("p (u a d) -> p d a u", u=2, d=D))
+        c_codes = const.tile([P, J], U32, align_bytes=64, name="c_codes")
+        c_scales = const.tile([P, J], U8, align_bytes=64, name="c_scales")
+        nc.vector.quantize_mx(out=c_codes[:].bitcast(FP8X4), scales=c_scales[:], in_=cg[:])
 
         def do_transposes(q):
             if q < NQ:
@@ -141,67 +152,78 @@ def tile_pnn_t_kernel(tc, x, centers, out):
                 products[q] = []
                 for i in range(QUAD):
                     mm = ps_m.tile([P, J], F32, tag="mm", name="mm")
-                    nc.tensor.matmul_mx(out=mm[:], lhsT=codes[:, i * P:(i + 1) * P].bitcast(FP8X4),
-                                        lhsT_scale=scales[:, i * P:(i + 1) * P],
+                    rows = slice(i * P, (i + 1) * P)
+                    nc.tensor.matmul_mx(out=mm[:], lhsT=codes[:, rows].bitcast(FP8X4), lhsT_scale=scales[:, rows],
                                         rhs=c_codes[:].bitcast(FP8X4), rhs_scale=c_scales[:], start=True, stop=True)
                     products[q].append(mm)
 
-        def units(q):
-            if q == NQ - 1:
-                return [(0, 2), (2, 2)]
-            return [(0, 4)]
+        def do_gram(q):
+            if q < NQ:
+                gm = ps_t.tile([P, 512], F32, tag="xt", name="gm")
+                for i in gram_tiles(q):
+                    for e in range(4):
+                        a = grouped[q][:, i * K + e:(i + 1) * K:4]
+                        nc.tensor.matmul(out=gm[:, i * P:(i + 1) * P], lhsT=a, rhs=a, start=(e == 0), stop=(e == 3))
+                grams[q] = gm
 
-        def do_logits(q):
-            if q >= NQ:
-                return
-            logits[q] = []
-            probs[q] = []
-            for (i0, n) in units(q):
-                t_sb = wpool.tile([P, n * J], F32, tag="t%d" % n, name="t_sb", bufs=(3 if n == QUAD else 4))
-                for i in range(n):
-                    t = q * QUAD + i0 + i
-                    nc.vector.scalar_tensor_tensor(out=t_sb[:, i * J:(i + 1) * J], in0=products[q][i0 + i][:],
-                                                   scalar=x2h[:, t:t + 1], in1=c2b[:], op0=ALU.subtract, op1=ALU.add)
-                logits[q].append(t_sb)
+        def do_diagonal(q):
+            if q < NQ:
+                for i in gram_tiles(q):
+                    t = q * QUAD + i
+                    dj = spool.tile([P, P], F32, tag="dj", name="dj")
+                    nc.vector.scalar_tensor_tensor(out=dj[:], in0=grams[q][:, i * P:(i + 1) * P], scalar=0.5,
+                                                   in1=ident[:], op0=ALU.mult, op1=ALU.mult, accum_out=x2h[:, t:t + 1])
+
+        def do_logit(q, i):
+            if 0 <= q < NQ:
+                if i == 0:
+                    logits[q] = wpool.tile([P, QUAD * J], F32, tag="t", name="t_sb", bufs=2)
+                t = q * QUAD + i
+                dst = logits[q][:].rearrange("p (d t o) -> p t d o", d=D, t=QUAD)[:, i]
+                nc.vector.scalar_tensor_tensor(out=dst, in0=products[q][i][:].rearrange("p (d o) -> p d o", d=D),
+                                               scalar=x2h[:, t:t + 1], in1=c2b[:].rearrange("p (d o) -> p d o", d=D),
+                                               op0=ALU.subtract, op1=ALU.add)
 
         def do_exp(q):
-            if q >= NQ:
-                return
-            for ui, (i0, n) in enumerate(units(q)):
-                p_sb = wpool.tile([P, n * J], F32, tag="p%d" % n, name="p_sb", bufs=(3 if n == QUAD else 4))
-                nc.scalar.activation(out=p_sb[:], in_=logits[q][ui][:], func=ACT.Exp)
-                probs[q].append(p_sb)
+            if 0 <= q < NQ:
+                p_sb = wpool.tile([P, QUAD * J], F32, tag="p", name="p_sb", bufs=3)
+                nc.scalar.activation(out=p_sb[:], in_=logits[q][:], func=ACT.Exp)
+                probs[q] = p_sb
 
-        def do_reduce(q):
-            maxes[q] = []
-            sums[q] = []
-            nu = len(units(q))
-            for ui, (i0, n) in enumerate(units(q)):
-                p3 = probs[q][ui][:].rearrange("p (g d) -> p g d", d=8)
-                mx = spool.tile([P, n * O], F32, tag="mx", name="mx", bufs=6)
-                nc.vector.tensor_reduce(out=mx[:], in_=p3, axis=AX.X, op=ALU.max)
-                l3 = spool.tile([P, n * O], F32, tag="l3", name="l3", bufs=6)
-                if nu > 1 and ui == nu - 1:
-                    nc.vector.tensor_reduce(out=l3[:], in_=p3, axis=AX.X, op=ALU.add)
-                else:
-                    l1 = spool.tile([P, n * O * 4], F32, tag="l1", name="l1", bufs=2)
-                    l1v = l1[:].rearrange("p (g d) -> p g d", d=4)
-                    nc.gpsimd.tensor_tensor(out=l1v, in0=p3[:, :, 0:4], in1=p3[:, :, 4:8], op=ALU.add)
-                    l2 = spool.tile([P, n * O * 2], F32, tag="l2", name="l2", bufs=2)
-                    l2v = l2[:].rearrange("p (g d) -> p g d", d=2)
-                    nc.gpsimd.tensor_tensor(out=l2v, in0=l1v[:, :, 0:2], in1=l1v[:, :, 2:4], op=ALU.add)
-                    l3v = l3[:].rearrange("p (g d) -> p g d", d=1)
-                    nc.gpsimd.tensor_tensor(out=l3v, in0=l2v[:, :, 0:1], in1=l2v[:, :, 1:2], op=ALU.add)
-                maxes[q].append(mx)
-                sums[q].append(l3)
+        def do_max(q, level):
+            if 0 <= q < NQ:
+                src = probs[q] if level == 0 else tops[q]
+                n = (4, 2, 1)[level] * W
+                dst = spool.tile([P, n], F32, tag="m%d" % level, name="m", bufs=2)
+                nc.vector.tensor_tensor(out=dst[:], in0=src[:, 0:n], in1=src[:, n:2 * n], op=ALU.max)
+                tops[q] = dst
+
+        def do_sum(q):
+            if 0 <= q < NQ:
+                ss = ps_s.tile([P, 512], F32, tag="ss", name="ss")
+                for h in range(2):
+                    for d in range(D):
+                        nc.tensor.matmul(out=ss[:, h * P:(h + 1) * P], lhsT=probs[q][:, d * W + h * P:d * W + (h + 1) * P],
+                                         rhs=ident[:], start=(d == 0), stop=(d == D - 1), is_transpose=True)
+                sums[q] = ss
+
+        def do_sum_copy(q):
+            if 0 <= q < NQ:
+                st = spool.tile([P, W], F32, tag="st", name="st", bufs=2)
+                nc.scalar.copy(out=st[:], in_=sums[q][:, 0:W])
+                sums[(q, 1)] = st
+
+        def do_sum_back(q):
+            if 0 <= q < NQ:
+                for h in range(2):
+                    nc.tensor.transpose(sums[q][:, W + h * P:W + (h + 1) * P], sums[(q, 1)][:, h * P:(h + 1) * P], ident[:])
 
         def do_final(q):
-            o_sb = spool.tile([P, QUAD * O], F32, tag="o", name="o_sb")
-            for ui, (i0, n) in enumerate(units(q)):
-                nc.vector.scalar_tensor_tensor(out=o_sb[:, i0 * O:(i0 + n) * O], in0=maxes[q][ui][:], scalar=9.0,
-                                               in1=sums[q][ui][:], op0=ALU.mult, op1=ALU.subtract)
-            w = QUAD * O
-            nc.sync.dma_start(out=ov[:, q * w:(q + 1) * w], in_=o_sb[:])
+            if 0 <= q < NQ:
+                o_sb = spool.tile([P, W], F32, tag="o", name="o_sb")
+                nc.vector.scalar_tensor_tensor(out=o_sb[:], in0=tops[q][:], scalar=9.0, in1=sums[q][:, W:2 * W],
+                                               op0=ALU.mult, op1=ALU.subtract)
+                nc.sync.dma_start(out=ov[:, q * W:(q + 1) * W], in_=o_sb[:])
 
         do_transposes(0)
         c_rep = const.tile([P, 4 * P], F32, name="c_rep")
@@ -213,26 +235,40 @@ def tile_pnn_t_kernel(tc, x, centers, out):
         norms_x(0)
         do_quantise(0)
         c2b = const.tile([P, J], F32, name="c2b")
-        nc.vector.tensor_scalar(out=c2b[:], in0=cb_ps[:], scalar1=-1.0, scalar2=-LN8, op0=ALU.mult, op1=ALU.add)
+        nc.vector.tensor_scalar(out=c2b[:].rearrange("p (d o) -> p d o", d=D), in0=cb_ps[:].rearrange("p (o d) -> p d o", d=D),
+                                scalar1=-1.0, scalar2=-LN8, op0=ALU.mult, op1=ALU.add)
+        do_gram(0)
         do_transposes(1)
         do_products(0)
+        do_diagonal(0)
         do_copies(1)
         norms_x(1)
-        do_logits(0)
+        for i in range(QUAD):
+            do_logit(0, i)
         do_quantise(1)
+        do_gram(1)
+        do_diagonal(1)
         do_transposes(2)
         do_products(1)
         do_copies(2)
 
-        for i in range(NQ + 3):
+        for i in range(NQ + 2):
             do_exp(i)
-            if 0 <= i - 1 < NQ:
-                do_reduce(i - 1)
-            if 0 <= i - 2 < NQ:
-                do_final(i - 2)
+            do_sum_copy(i - 1)
+            do_max(i - 1, 0)
+            do_logit(i + 1, 0)
+            do_max(i - 1, 1)
+            do_logit(i + 1, 1)
+            do_max(i - 1, 2)
+            do_logit(i + 1, 2)
             do_quantise(i + 2)
-            do_logits(i + 1)
+            do_logit(i + 1, 3)
+            do_gram(i + 2)
             do_transposes(i + CP_AHEAD)
+            do_sum_back(i - 1)
             do_products(i + 2)
+            do_sum(i)
+            do_diagonal(i + 2)
+            do_final(i - 1)
             do_copies(i + CP_AHEAD)
             norms_x(i + X2_AHEAD)

@@ -28,6 +28,7 @@ GRAM_EVEN = [3]
 GRAM_ODD = [3]
 VC = (0, 1)
 VC2 = ()
+SS_TO = 13
 
 
 def gram_tiles(q):
@@ -118,6 +119,7 @@ def tile_pnn_t_kernel(tc, x, centers, out):
         probs = {}
         tops = {}
         sums = {}
+        top2 = {}
 
         half_norms(c_sb[:], c2h, range(4))
         c_banks = transposes(c_sb[:])
@@ -146,16 +148,15 @@ def tile_pnn_t_kernel(tc, x, centers, out):
                 nc.vector.quantize_mx(out=codes[:].bitcast(FP8X4), scales=scales[:], in_=grouped[q][:])
                 packed[q] = (codes, scales)
 
-        def do_products(q):
+        def do_products(q, tiles=range(QUAD)):
             if q < NQ:
                 codes, scales = packed[q]
-                products[q] = []
-                for i in range(QUAD):
+                for i in tiles:
                     mm = ps_m.tile([P, J], F32, tag="mm", name="mm")
                     rows = slice(i * P, (i + 1) * P)
                     nc.tensor.matmul_mx(out=mm[:], lhsT=codes[:, rows].bitcast(FP8X4), lhsT_scale=scales[:, rows],
                                         rhs=c_codes[:].bitcast(FP8X4), rhs_scale=c_scales[:], start=True, stop=True)
-                    products[q].append(mm)
+                    products[(q, i)] = mm
 
         def do_gram(q):
             if q < NQ:
@@ -180,37 +181,67 @@ def tile_pnn_t_kernel(tc, x, centers, out):
                     logits[q] = wpool.tile([P, QUAD * J], F32, tag="t", name="t_sb", bufs=2)
                 t = q * QUAD + i
                 dst = logits[q][:].rearrange("p (d t o) -> p t d o", d=D, t=QUAD)[:, i]
-                nc.vector.scalar_tensor_tensor(out=dst, in0=products[q][i][:].rearrange("p (d o) -> p d o", d=D),
+                nc.vector.scalar_tensor_tensor(out=dst, in0=products[(q, i)][:].rearrange("p (d o) -> p d o", d=D),
                                                scalar=x2h[:, t:t + 1], in1=c2b[:].rearrange("p (d o) -> p d o", d=D),
                                                op0=ALU.subtract, op1=ALU.add)
 
         def do_exp(q):
             if 0 <= q < NQ:
                 p_sb = wpool.tile([P, QUAD * J], F32, tag="p", name="p_sb", bufs=3)
-                nc.scalar.activation(out=p_sb[:], in_=logits[q][:], func=ACT.Exp)
+                if q < NQ - 1:
+                    nc.scalar.activation(out=p_sb[:], in_=logits[q][:], func=ACT.Exp)
+                else:
+                    for h in range(2):
+                        nc.scalar.activation(out=pair(p_sb, h), in_=pair(logits[q], h), func=ACT.Exp)
                 probs[q] = p_sb
+
+        def pair(tile, h, n=D):
+            return tile[:].rearrange("p (d w) -> p d w", w=W)[:, :, h * P:(h + 1) * P]
+
+        def do_pair_max(q, h, n):
+            top = pair(probs[q], h) if n == 4 else tops[(q, h)]
+            m = spool.tile([P, n * P], F32, tag="hm%d" % n, name="m", bufs=2)
+            mv = m[:].rearrange("p (d w) -> p d w", w=P)
+            nc.vector.tensor_tensor(out=mv, in0=top[:, 0:n], in1=top[:, n:2 * n], op=ALU.max)
+            tops[(q, h)] = mv
+
+        def do_pair_final(q, h):
+            o_sb = spool.tile([P, P], F32, tag="oh", name="o_sb")
+            nc.vector.scalar_tensor_tensor(out=o_sb[:], in0=tops[(q, h)][:, 0], scalar=9.0,
+                                           in1=sums[q][:, W + h * P:W + (h + 1) * P],
+                                           op0=ALU.mult, op1=ALU.subtract)
+            nc.sync.dma_start(out=ov[:, q * W + h * P:q * W + (h + 1) * P], in_=o_sb[:])
 
         def do_max(q, level):
             if 0 <= q < NQ:
                 src = probs[q] if level == 0 else tops[q]
                 n = (4, 2, 1)[level] * W
-                dst = spool.tile([P, n], F32, tag="m%d" % level, name="m", bufs=2)
+                dst = spool.tile([P, n], F32, tag="m%d" % level, name="m", bufs=(3 if level == 2 else 2))
                 nc.vector.tensor_tensor(out=dst[:], in0=src[:, 0:n], in1=src[:, n:2 * n], op=ALU.max)
                 tops[q] = dst
+                if level == 2:
+                    top2[q] = dst
 
-        def do_sum(q):
+        def do_sum(q, pairs=range(2)):
             if 0 <= q < NQ:
-                ss = ps_s.tile([P, 512], F32, tag="ss", name="ss")
-                for h in range(2):
+                if q not in sums:
+                    if q < SS_TO:
+                        sums[q] = ps_s.tile([P, 512], F32, tag="ss", name="ss")
+                    else:
+                        sums[q] = ps_m.tile([P, 512], F32, tag="mm", name="ss")
+                for h in pairs:
                     for d in range(D):
-                        nc.tensor.matmul(out=ss[:, h * P:(h + 1) * P], lhsT=probs[q][:, d * W + h * P:d * W + (h + 1) * P],
+                        nc.tensor.matmul(out=sums[q][:, h * P:(h + 1) * P], lhsT=probs[q][:, d * W + h * P:d * W + (h + 1) * P],
                                          rhs=ident[:], start=(d == 0), stop=(d == D - 1), is_transpose=True)
-                sums[q] = ss
 
         def do_sum_copy(q):
             if 0 <= q < NQ:
-                st = spool.tile([P, W], F32, tag="st", name="st", bufs=2)
-                nc.scalar.copy(out=st[:], in_=sums[q][:, 0:W])
+                st = spool.tile([P, W], F32, tag="st", name="st", bufs=3)
+                if q < NQ - 1:
+                    nc.scalar.copy(out=st[:], in_=sums[q][:, 0:W])
+                else:
+                    for h in range(2):
+                        nc.scalar.copy(out=st[:, h * P:(h + 1) * P], in_=sums[q][:, h * P:(h + 1) * P])
                 sums[(q, 1)] = st
 
         def do_sum_back(q):
@@ -221,7 +252,7 @@ def tile_pnn_t_kernel(tc, x, centers, out):
         def do_final(q):
             if 0 <= q < NQ:
                 o_sb = spool.tile([P, W], F32, tag="o", name="o_sb")
-                nc.vector.scalar_tensor_tensor(out=o_sb[:], in0=tops[q][:], scalar=9.0, in1=sums[q][:, W:2 * W],
+                nc.vector.scalar_tensor_tensor(out=o_sb[:], in0=top2[q][:], scalar=9.0, in1=sums[q][:, W:2 * W],
                                                op0=ALU.mult, op1=ALU.subtract)
                 nc.sync.dma_start(out=ov[:, q * W:(q + 1) * W], in_=o_sb[:])
 
@@ -252,7 +283,7 @@ def tile_pnn_t_kernel(tc, x, centers, out):
         do_products(1)
         do_copies(2)
 
-        for i in range(NQ + 2):
+        for i in range(NQ - 2):
             do_exp(i)
             do_sum_copy(i - 1)
             do_max(i - 1, 0)
@@ -263,8 +294,8 @@ def tile_pnn_t_kernel(tc, x, centers, out):
             do_logit(i + 1, 2)
             do_quantise(i + 2)
             do_logit(i + 1, 3)
-            do_gram(i + 2)
             do_transposes(i + CP_AHEAD)
+            do_gram(i + 2)
             do_sum_back(i - 1)
             do_products(i + 2)
             do_sum(i)
@@ -272,3 +303,33 @@ def tile_pnn_t_kernel(tc, x, centers, out):
             do_final(i - 1)
             do_copies(i + CP_AHEAD)
             norms_x(i + X2_AHEAD)
+
+        q = NQ - 2
+        do_exp(q)
+        do_sum_copy(q - 1)
+        for t in range(QUAD):
+            do_logit(q + 1, t)
+        do_sum_back(q - 1)
+        do_exp(q + 1)
+        do_sum(q)
+        do_max(q - 1, 0)
+        do_max(q, 0)
+        do_max(q - 1, 1)
+        do_max(q, 1)
+        do_max(q - 1, 2)
+        do_max(q, 2)
+        do_final(q - 1)
+        do_sum_copy(q)
+        do_sum_back(q)
+        do_sum(q + 1)
+        do_sum_copy(q + 1)
+        do_pair_max(q + 1, 0, 4)
+        do_pair_max(q + 1, 1, 4)
+        do_pair_max(q + 1, 0, 2)
+        do_pair_max(q + 1, 1, 2)
+        do_final(q)
+        do_pair_max(q + 1, 0, 1)
+        do_pair_max(q + 1, 1, 1)
+        do_sum_back(q + 1)
+        do_pair_final(q + 1, 0)
+        do_pair_final(q + 1, 1)

import math
from contextlib import ExitStack

import concourse.mybir as mybir
from concourse.masks import make_identity

F32 = mybir.dt.float32
BF16 = mybir.dt.bfloat16
U32 = mybir.dt.uint32
U8 = mybir.dt.uint8
FP8X4 = mybir.dt.float8_e4m3fn_x4
ALU = mybir.AluOpType
ACT = mybir.ActivationFunctionType

P = 128
B, K, J, O, D = 8192, 512, 512, 64, 8
NT = B // P
QUAD = 4
NQ = NT // QUAD
W = QUAD * O
FLOPS = 2 * B * K * J
LN8 = math.log(8.0)
RH = math.sqrt(0.5)
CHUNKS = [4, 4, 8, 8, 8, 8, 8, 8, 8]
CP_AHEAD = 3
X2_AHEAD = 2
GRAM_EVEN = [3]
GRAM_ODD = [3]
VC = (0, 1)
VC2 = ()
SS_TO = 13


def gram_tiles(q):
    return GRAM_EVEN if q % 2 == 0 else GRAM_ODD


def vector_copies(q, h):
    return (h == 0 and q in VC) or (h == 1 and q in VC2)


def tile_pnn_t_kernel(tc, x, centers, out):
    nc = tc.nc
    xv = x.rearrange("(p t) k -> p (t k)", t=NT)
    cv = centers.rearrange("o d k -> (o d) k").rearrange("(i r) k -> r i k", r=P)
    ov = out.rearrange("(p t) o -> p (t o)", t=NT)

    with ExitStack() as ctx:
        ctx.enter_context(tc.manual_schedule())
        const = ctx.enter_context(tc.tile_pool(name="const", bufs=1))
        xpool = ctx.enter_context(tc.tile_pool(name="xpool", bufs=1))
        gpool = ctx.enter_context(tc.tile_pool(name="gpool", bufs=3))
        wpool = ctx.enter_context(tc.tile_pool(name="wpool", bufs=3))
        spool = ctx.enter_context(tc.tile_pool(name="spool", bufs=3))
        ps_t = ctx.enter_context(tc.psum_pool(name="ps_t", bufs=3))
        ps_m = ctx.enter_context(tc.psum_pool(name="ps_m", bufs=4))
        ps_s = ctx.enter_context(tc.psum_pool(name="ps_s", bufs=1))

        c_sb = const.tile([P, 4 * K], BF16, name="c_sb")
        for h in range(2):
            nc.sync.dma_start(out=c_sb[:, h * 2 * K:(h + 1) * 2 * K].rearrange("r (i k) -> r i k", i=2),
                              in_=cv[:, 2 * h:2 * h + 2, :])
        quad_src = []
        t0 = 0
        for ci, n in enumerate(CHUNKS):
            xc = xpool.tile([P, n * K], BF16, name="x%d" % ci)
            nc.sync.dma_start(out=xc[:], in_=xv[:, t0 * K:(t0 + n) * K])
            for h in range(n // QUAD):
                quad_src.append(xc[:, h * QUAD * K:(h + 1) * QUAD * K])
            t0 += n

        ident = const.tile([P, P], F32, name="ident")
        make_identity(nc, ident[:])
        ones = const.tile([P, P], F32, name="ones")
        nc.vector.memset(ones[:], 1.0)
        x2h = const.tile([P, NT], F32, name="x2h")
        c2h = const.tile([P, 4], F32, name="c2h")

        def transposes(src):
            src32 = src.bitcast(F32)
            banks = []
            for h in range(2):
                xt = ps_t.tile([P, 512], F32, tag="xt", name="xt")
                for c in range(2):
                    for u in range(2):
                        col = (2 * h + c) * 256 + u * P
                        nc.tensor.transpose(xt[:, (2 * c + u) * P:(2 * c + u + 1) * P], src32[:, col:col + P], ident[:])
                banks.append(xt)
            return banks

        def copies(banks, on_vector):
            g = gpool.tile([P, QUAD * K], BF16, align_bytes=64, tag="g", name="g")
            g32 = g[:].bitcast(F32)
            for h in range(2):
                dst = g32[:, h * 512:(h + 1) * 512].rearrange("p (c b u) -> p c b u", c=2, u=2)
                srcv = banks[h][:].rearrange("p (c u b) -> p c b u", c=2, u=2)
                if on_vector[h]:
                    nc.vector.tensor_copy(out=dst, in_=srcv)
                else:
                    nc.scalar.copy(out=dst, in_=srcv)
            return g

        def half_norms(src, dest, tiles):
            for i in tiles:
                junk = spool.tile([P, K], BF16, tag="junk", name="junk")
                nc.scalar.activation(out=junk[:], in_=src[:, i * K:(i + 1) * K], func=ACT.Square, scale=RH,
                                     accum_out=dest[:, i:i + 1])

        def norms_x(q):
            if q < NQ:
                half_norms(quad_src[q], x2h[:, q * QUAD:(q + 1) * QUAD], [i for i in range(QUAD) if i not in gram_tiles(q)])

        banks = {}
        grouped = {}
        packed = {}
        products = {}
        grams = {}
        logits = {}
        probs = {}
        tops = {}
        sums = {}
        top2 = {}

        half_norms(c_sb[:], c2h, range(4))
        c_banks = transposes(c_sb[:])
        cg = gpool.tile([P, QUAD * K], BF16, align_bytes=64, tag="g", name="cg")
        cg_v = cg[:].bitcast(F32).rearrange("p (d c a u) -> p c d a u", d=D, c=4, u=2)
        for c in range(4):
            nc.vector.tensor_copy(
                out=cg_v[:, c],
                in_=c_banks[c // 2][:, (c % 2) * 256:(c % 2 + 1) * 256].rearrange("p (u a d) -> p d a u", u=2, d=D))
        c_codes = const.tile([P, J], U32, align_bytes=64, name="c_codes")
        c_scales = const.tile([P, J], U8, align_bytes=64, name="c_scales")
        nc.vector.quantize_mx(out=c_codes[:].bitcast(FP8X4), scales=c_scales[:], in_=cg[:])

        def do_transposes(q):
            if q < NQ:
                banks[q] = transposes(quad_src[q])

        def do_copies(q):
            if q < NQ:
                grouped[q] = copies(banks[q], [vector_copies(q, 0), vector_copies(q, 1)])

        def do_quantise(q):
            if q < NQ:
                codes = wpool.tile([P, QUAD * P], U32, align_bytes=64, tag="codes", name="codes")
                scales = wpool.tile([P, QUAD * P], U8, align_bytes=64, tag="scales", name="scales")
                nc.vector.quantize_mx(out=codes[:].bitcast(FP8X4), scales=scales[:], in_=grouped[q][:])
                packed[q] = (codes, scales)

        def do_products(q, tiles=range(QUAD)):
            if q < NQ:
                codes, scales = packed[q]
                for i in tiles:
                    mm = ps_m.tile([P, J], F32, tag="mm", name="mm")
                    rows = slice(i * P, (i + 1) * P)
                    nc.tensor.matmul_mx(out=mm[:], lhsT=codes[:, rows].bitcast(FP8X4), lhsT_scale=scales[:, rows],
                                        rhs=c_codes[:].bitcast(FP8X4), rhs_scale=c_scales[:], start=True, stop=True)
                    products[(q, i)] = mm

        def do_gram(q):
            if q < NQ:
                gm = ps_t.tile([P, 512], F32, tag="xt", name="gm")
                for i in gram_tiles(q):
                    for e in range(4):
                        a = grouped[q][:, i * K + e:(i + 1) * K:4]
                        nc.tensor.matmul(out=gm[:, i * P:(i + 1) * P], lhsT=a, rhs=a, start=(e == 0), stop=(e == 3))
                grams[q] = gm

        def do_diagonal(q):
            if q < NQ:
                for i in gram_tiles(q):
                    t = q * QUAD + i
                    dj = spool.tile([P, P], F32, tag="dj", name="dj")
                    nc.vector.scalar_tensor_tensor(out=dj[:], in0=grams[q][:, i * P:(i + 1) * P], scalar=0.5,
                                                   in1=ident[:], op0=ALU.mult, op1=ALU.mult, accum_out=x2h[:, t:t + 1])

        def do_logit(q, i):
            if 0 <= q < NQ:
                if i == 0:
                    logits[q] = wpool.tile([P, QUAD * J], F32, tag="t", name="t_sb", bufs=2)
                t = q * QUAD + i
                dst = logits[q][:].rearrange("p (d t o) -> p t d o", d=D, t=QUAD)[:, i]
                nc.vector.scalar_tensor_tensor(out=dst, in0=products[(q, i)][:].rearrange("p (d o) -> p d o", d=D),
                                               scalar=x2h[:, t:t + 1], in1=c2b[:].rearrange("p (d o) -> p d o", d=D),
                                               op0=ALU.subtract, op1=ALU.add)

        def do_exp(q):
            if 0 <= q < NQ:
                p_sb = wpool.tile([P, QUAD * J], F32, tag="p", name="p_sb", bufs=3)
                if q < NQ - 1:
                    nc.scalar.activation(out=p_sb[:], in_=logits[q][:], func=ACT.Exp)
                else:
                    for h in range(2):
                        nc.scalar.activation(out=pair(p_sb, h), in_=pair(logits[q], h), func=ACT.Exp)
                probs[q] = p_sb

        def pair(tile, h, n=D):
            return tile[:].rearrange("p (d w) -> p d w", w=W)[:, :, h * P:(h + 1) * P]

        def do_pair_max(q, h, n):
            top = pair(probs[q], h) if n == 4 else tops[(q, h)]
            m = spool.tile([P, n * P], F32, tag="hm%d" % n, name="m", bufs=2)
            mv = m[:].rearrange("p (d w) -> p d w", w=P)
            nc.vector.tensor_tensor(out=mv, in0=top[:, 0:n], in1=top[:, n:2 * n], op=ALU.max)
            tops[(q, h)] = mv

        def do_pair_final(q, h):
            o_sb = spool.tile([P, P], F32, tag="oh", name="o_sb")
            nc.vector.scalar_tensor_tensor(out=o_sb[:], in0=tops[(q, h)][:, 0], scalar=9.0,
                                           in1=sums[q][:, W + h * P:W + (h + 1) * P],
                                           op0=ALU.mult, op1=ALU.subtract)
            nc.sync.dma_start(out=ov[:, q * W + h * P:q * W + (h + 1) * P], in_=o_sb[:])

        def do_max(q, level):
            if 0 <= q < NQ:
                src = probs[q] if level == 0 else tops[q]
                n = (4, 2, 1)[level] * W
                dst = spool.tile([P, n], F32, tag="m%d" % level, name="m", bufs=(3 if level == 2 else 2))
                nc.vector.tensor_tensor(out=dst[:], in0=src[:, 0:n], in1=src[:, n:2 * n], op=ALU.max)
                tops[q] = dst
                if level == 2:
                    top2[q] = dst

        def do_sum(q, pairs=range(2)):
            if 0 <= q < NQ:
                if q not in sums:
                    if q < SS_TO:
                        sums[q] = ps_s.tile([P, 512], F32, tag="ss", name="ss")
                    else:
                        sums[q] = ps_m.tile([P, 512], F32, tag="mm", name="ss")
                for h in pairs:
                    for d in range(D):
                        nc.tensor.matmul(out=sums[q][:, h * P:(h + 1) * P], lhsT=probs[q][:, d * W + h * P:d * W + (h + 1) * P],
                                         rhs=ident[:], start=(d == 0), stop=(d == D - 1), is_transpose=True)

        def do_sum_copy(q):
            if 0 <= q < NQ:
                st = spool.tile([P, W], F32, tag="st", name="st", bufs=3)
                if q < NQ - 1:
                    nc.scalar.copy(out=st[:], in_=sums[q][:, 0:W])
                else:
                    for h in range(2):
                        nc.scalar.copy(out=st[:, h * P:(h + 1) * P], in_=sums[q][:, h * P:(h + 1) * P])
                sums[(q, 1)] = st

        def do_sum_back(q):
            if 0 <= q < NQ:
                for h in range(2):
                    nc.tensor.transpose(sums[q][:, W + h * P:W + (h + 1) * P], sums[(q, 1)][:, h * P:(h + 1) * P], ident[:])

        def do_final(q):
            if 0 <= q < NQ:
                o_sb = spool.tile([P, W], F32, tag="o", name="o_sb")
                nc.vector.scalar_tensor_tensor(out=o_sb[:], in0=top2[q][:], scalar=9.0, in1=sums[q][:, W:2 * W],
                                               op0=ALU.mult, op1=ALU.subtract)
                nc.sync.dma_start(out=ov[:, q * W:(q + 1) * W], in_=o_sb[:])

        do_transposes(0)
        c_rep = const.tile([P, 4 * P], F32, name="c_rep")
        cb_ps = ps_m.tile([P, J], F32, tag="mm", name="cb_ps")
        for i in range(4):
            nc.vector.tensor_scalar_mul(out=c_rep[:, i * P:(i + 1) * P], in0=ones[:], scalar1=c2h[:, i:i + 1])
            nc.tensor.transpose(cb_ps[:, i * P:(i + 1) * P], c_rep[:, i * P:(i + 1) * P], ident[:])
        do_copies(0)
        norms_x(0)
        do_quantise(0)
        c2b = const.tile([P, J], F32, name="c2b")
        nc.vector.tensor_scalar(out=c2b[:].rearrange("p (d o) -> p d o", d=D), in0=cb_ps[:].rearrange("p (o d) -> p d o", d=D),
                                scalar1=-1.0, scalar2=-LN8, op0=ALU.mult, op1=ALU.add)
        do_gram(0)
        do_transposes(1)
        do_products(0)
        do_diagonal(0)
        do_copies(1)
        norms_x(1)
        for i in range(QUAD):
            do_logit(0, i)
        do_quantise(1)
        do_gram(1)
        do_diagonal(1)
        do_transposes(2)
        do_products(1)
        do_copies(2)

        for i in range(NQ - 2):
            do_exp(i)
            do_sum_copy(i - 1)
            do_max(i - 1, 0)
            do_logit(i + 1, 0)
            do_max(i - 1, 1)
            do_logit(i + 1, 1)
            do_max(i - 1, 2)
            do_logit(i + 1, 2)
            do_quantise(i + 2)
            do_logit(i + 1, 3)
            do_transposes(i + CP_AHEAD)
            do_gram(i + 2)
            do_sum_back(i - 1)
            do_products(i + 2)
            do_sum(i)
            do_diagonal(i + 2)
            do_final(i - 1)
            do_copies(i + CP_AHEAD)
            norms_x(i + X2_AHEAD)

        q = NQ - 2
        do_exp(q)
        do_sum_copy(q - 1)
        for t in range(QUAD):
            do_logit(q + 1, t)
        do_sum_back(q - 1)
        do_exp(q + 1)
        do_sum(q)
        do_max(q - 1, 0)
        do_max(q, 0)
        do_max(q - 1, 1)
        do_max(q, 1)
        do_max(q - 1, 2)
        do_max(q, 2)
        do_final(q - 1)
        do_sum_copy(q)
        do_sum_back(q)
        do_sum(q + 1)
        do_sum_copy(q + 1)
        do_pair_max(q + 1, 0, 4)
        do_pair_max(q + 1, 1, 4)
        do_pair_max(q + 1, 0, 2)
        do_pair_max(q + 1, 1, 2)
        do_final(q)
        do_pair_max(q + 1, 0, 1)
        do_pair_max(q + 1, 1, 1)
        do_sum_back(q + 1)
        do_pair_final(q + 1, 0)
        do_pair_final(q + 1, 1)
